import numpy as np
import ml_dtypes


def mxq(x, axis, fmt="e4m3"):
    dtype, down = {"e4m3": (ml_dtypes.float8_e4m3fn, 7), "e5m2": (ml_dtypes.float8_e5m2, 14)}[fmt]
    v = np.moveaxis(np.asarray(x, np.float32).astype(ml_dtypes.bfloat16).astype(np.float64), axis, -1)
    blocks = v.reshape(v.shape[:-1] + (-1, 32))
    amax = np.abs(blocks).max(-1, keepdims=True)
    byte = np.maximum(np.where(amax > 0, np.frexp(amax)[1] - 1 + 127, 0) - down, 1)
    scale = np.exp2(byte - 127.0)
    codes = (blocks / scale).astype(np.float32).astype(dtype).astype(np.float64)
    return np.moveaxis((codes * scale).reshape(v.shape), -1, axis)


WIDE = False


def mx_kscale(k):
    if not WIDE:
        return np.ones(k)
    levels = np.array([10, -10, 5, -5, 0])
    a = np.random.permutation(np.resize(levels, k // 512 * 4)).reshape(k // 512, 4)
    idx = np.arange(k)
    return np.exp2(a[idx // 512, idx % 128 // 32])


BF16 = ml_dtypes.bfloat16


def bf(x):
    return np.asarray(x, np.float32).astype(BF16)


def f64(x):
    return np.asarray(x).astype(np.float64)


B, I, J, K, D = 4096, 256, 1024, 4, 2


def squash(x, axis=-1):
    norm = np.sqrt(np.sum(x * x, axis=axis, keepdims=True))
    scale = norm ** 2 / (1.0 + norm ** 2) / (norm + 1e-8)
    return scale * x


def setup_inputs():
    s = mx_kscale(J)
    c = 2.0 / np.sqrt(J * D * (K * K / 4.0 + K / 12.0))
    return {"X": bf(np.random.standard_normal((B, J, D)) * s[None, :, None]),
            "weight": bf(np.random.random((I, J, K, D)) * c / s[None, :, None, None])}


def reference(X, weight):
    xq = mxq(f64(X), 1, "e4m3")
    wq = mxq(f64(weight).sum(axis=2), 1, "e4m3")
    s = xq.transpose(2, 0, 1) @ wq.transpose(2, 1, 0)
    return squash(s.transpose(1, 2, 0), axis=-1)

@@ -1,0 +1,171 @@
+from contextlib import ExitStack
+
+import concourse.mybir as mybir
+from concourse.masks import make_identity
+
+F32 = mybir.dt.float32
+BF16 = mybir.dt.bfloat16
+U32 = mybir.dt.uint32
+U8 = mybir.dt.uint8
+FP8X4 = mybir.dt.float8_e4m3fn_x4
+ACT = mybir.ActivationFunctionType
+ALU = mybir.AluOpType
+
+B, I, J, K, D = 4096, 256, 1024, 4, 2
+P = 128
+FLOPS = 2 * B * I * J * D
+ROWS = 4
+NT = B // P
+EPS = 1e-8
+TINY = 1e-30
+VEC_BANKS = (3,)
+
+
+def tile_primary_capsule_t_kernel(tc, X, weight, out):
+    nc = tc.nc
+    Xv = X.rearrange("(T p r) j d -> T p r (j d)", p=P, r=ROWS)
+    Wv = weight.rearrange("(t p) j k d -> t p (j k d)", p=P)
+    Ov = out.rearrange("(T p r) i d -> T p r (i d)", p=P, r=ROWS)
+    with ExitStack() as ctx:
+        const = ctx.enter_context(tc.tile_pool(name="const", bufs=1))
+        xin = ctx.enter_context(tc.tile_pool(name="xin", bufs=3))
+        wtmp = ctx.enter_context(tc.tile_pool(name="wtmp", bufs=2))
+        grp = ctx.enter_context(tc.tile_pool(name="grp", bufs=4))
+        xqp = ctx.enter_context(tc.tile_pool(name="xqp", bufs=8))
+        ep = ctx.enter_context(tc.tile_pool(name="ep", bufs=3))
+        tp = ctx.enter_context(tc.psum_pool(name="tp", bufs=4))
+        accp = ctx.enter_context(tc.psum_pool(name="accp", bufs=4))
+
+        warm = const.tile([P, 1], F32, name="warm")
+        nc.vector.memset(warm[:], 1.0)
+        nc.scalar.activation(out=warm[:], in_=warm[:], func=ACT.Abs_reciprocal_sqrt)
+
+        ident_f = const.tile([P, P], F32, name="ident_f")
+        make_identity(nc, ident_f[:])
+        ident_b = const.tile([P, P], BF16, name="ident_b")
+        make_identity(nc, ident_b[:])
+
+        x_tiles = {}
+
+        def load_x(T, split):
+            x_sb = xin.tile([P, ROWS, J * D], BF16, name="x_sb")
+            if split:
+                for r in range(ROWS):
+                    nc.sync.dma_start(out=x_sb[:, r, :], in_=Xv[T][:, r, :])
+            else:
+                nc.sync.dma_start(out=x_sb[:], in_=Xv[T])
+            x_tiles[T] = x_sb
+
+        load_x(0, True)
+        w_raw = [const.tile([P, J * K * D], BF16, name="w_raw%d" % t) for t in range(2)]
+        HALF = J * K * D // 2
+        for g in range(2):
+            for t in range(2):
+                nc.sync.dma_start(out=w_raw[t][:, g * HALF:(g + 1) * HALF],
+                                  in_=Wv[t][:, g * HALF:(g + 1) * HALF])
+        load_x(1, False)
+
+        bank_no = [0]
+
+        def copy_out(dst, src):
+            if bank_no[0] % 8 in VEC_BANKS:
+                nc.vector.tensor_copy(out=dst, in_=src)
+            else:
+                nc.scalar.copy(out=dst, in_=src)
+            bank_no[0] += 1
+
+        xq_tiles = {}
+
+        def front(n):
+            T, r = divmod(n, ROWS)
+            xw = x_tiles[T][:, r, :].bitcast(F32)
+            gx = grp.tile([P, 2, D, P, 4], BF16, name="gx", align_bytes=64)
+            for g in range(2):
+                xt = tp.tile([P, 4, P], F32, name="xt", tag="tp")
+                for u in range(4):
+                    c = 4 * g + u
+                    nc.tensor.transpose(xt[:, u, :], xw[:, c * P:(c + 1) * P], ident_f[:])
+                copy_out(gx[:, g], xt[:].bitcast(BF16).rearrange("p u (b d) -> p d b u", d=D))
+            xq = xqp.tile([P, 4 * P], U32, name="xq", align_bytes=64)
+            xs = xqp.tile([P, 4 * P], U8, name="xs", align_bytes=64)
+            nc.vector.quantize_mx(out=xq[:].bitcast(FP8X4), scales=xs[:],
+                                  in_=gx[:].rearrange("p g d b t -> p (g d b t)"))
+            xq_tiles[n] = (xq, xs)
+
+        front(0)
+        front(1)
+
+        ws = [const.tile([P, D, J], BF16, name="ws%d" % t) for t in range(2)]
+        gw = const.tile([P, 2, D, I, 4], BF16, name="gw", align_bytes=64)
+        wq = const.tile([P, 4 * I], U32, name="wq", align_bytes=64)
+        wsc = const.tile([P, 4 * I], U8, name="wsc", align_bytes=64)
+        JH = J // 2
+        for g in range(2):
+            for t in range(2):
+                w4 = w_raw[t][:, g * HALF:(g + 1) * HALF].rearrange("p (j h c) -> p j h c", h=2, c=4)
+                part = wtmp.tile([P, JH, 4], F32, name="part")
+                nc.vector.tensor_tensor(out=part[:], in0=w4[:, :, 0, :], in1=w4[:, :, 1, :], op=ALU.add)
+                pv = part[:].rearrange("p j (e d) -> p d j e", d=D)
+                nc.vector.tensor_tensor(out=ws[t][:, :, g * JH:(g + 1) * JH], in0=pv[:, :, :, 0],
+                                        in1=pv[:, :, :, 1], op=ALU.add)
+                for d in range(D):
+                    wt = tp.tile([P, 4, P], BF16, name="wt", tag="tp")
+                    for u in range(4):
+                        c = 4 * g + u
+                        nc.tensor.transpose(wt[:, u, :], ws[t][:, d, c * P:(c + 1) * P], ident_b[:])
+                    nc.scalar.copy(out=gw[:, g, d, t * P:(t + 1) * P, :],
+                                   in_=wt[:].rearrange("p u i -> p i u"))
+            nc.vector.quantize_mx(out=wq[:, g * 2 * I:(g + 1) * 2 * I].bitcast(FP8X4),
+                                  scales=wsc[:, g * 2 * I:(g + 1) * 2 * I],
+                                  in_=gw[:, g].rearrange("p d i t -> p (d i t)"))
+
+        def mx(n):
+            xq, xs = xq_tiles[n]
+            acc = accp.tile([P, D, I], F32, name="acc")
+            for d in range(D):
+                for g in range(2):
+                    cx = (2 * g + d) * P
+                    cw = (2 * g + d) * I
+                    nc.tensor.matmul_mx(out=acc[:, d, :],
+                                        lhsT=xq[:, cx:cx + P].bitcast(FP8X4),
+                                        lhsT_scale=xs[:, cx:cx + P],
+                                        rhs=wq[:, cw:cw + I].bitcast(FP8X4),
+                                        rhs_scale=wsc[:, cw:cw + I],
+                                        start=(g == 0), stop=(g == 1))
+            return acc
+
+        def epilogue(m, accs):
+            T, h = divmod(m, 2)
+            sq = ep.tile([P, 2, D, I], F32, name="sq")
+            for e in range(2):
+                nc.scalar.activation(out=sq[:, e], in_=accs[e][:], func=ACT.Square)
+            n2 = ep.tile([P, 2, I], F32, name="n2")
+            nc.vector.tensor_tensor(out=n2[:], in0=sq[:, :, 0, :], in1=sq[:, :, 1, :], op=ALU.add)
+            nn = ep.tile([P, 2, I], F32, name="nn")
+            nc.scalar.activation(out=nn[:], in_=n2[:], func=ACT.Abs_reciprocal_sqrt, bias=TINY, scale=1.0)
+            nc.vector.tensor_tensor(out=nn[:], in0=n2[:], in1=nn[:], op=ALU.mult)
+            den = ep.tile([P, 2, I], F32, name="den")
+            nc.vector.tensor_scalar_add(out=den[:], in0=n2[:], scalar1=1.0)
+            nc.vector.scalar_tensor_tensor(out=den[:].rearrange("p e i -> p (e i)"),
+                                           in0=nn[:].rearrange("p e i -> p (e i)"), scalar=EPS,
+                                           in1=den[:].rearrange("p e i -> p (e i)"),
+                                           op0=ALU.add, op1=ALU.mult)
+            rr = ep.tile([P, 2, I], F32, name="rr")
+            nc.scalar.activation(out=rr[:], in_=den[:], func=ACT.Abs_reciprocal_sqrt)
+            nc.scalar.activation(out=rr[:], in_=rr[:], func=ACT.Square)
+            nc.vector.tensor_tensor(out=rr[:], in0=n2[:], in1=rr[:], op=ALU.mult)
+            o_sb = ep.tile([P, 2, I, D], F32, name="o_sb")
+            for e in range(2):
+                nc.vector.tensor_tensor(out=o_sb[:, e], in0=accs[e][:].rearrange("p d i -> p i d"),
+                                        in1=rr[:, e, :].unsqueeze(2).to_broadcast([P, I, D]), op=ALU.mult)
+            nc.sync.dma_start(out=Ov[T][:, 2 * h:2 * h + 2, :],
+                              in_=o_sb[:].rearrange("p e i d -> p e (i d)"))
+
+        for m in range(NT // 2):
+            for n in (2 * m + 2, 2 * m + 3):
+                if n < NT:
+                    if n % ROWS == 0 and n // ROWS + 1 < NT // ROWS:
+                        load_x(n // ROWS + 1, False)
+                    front(n)
+            accs = [mx(2 * m), mx(2 * m + 1)]
+            epilogue(m, accs)

@@ -14,158 +14,197 @@ ALU = mybir.AluOpType
 B, I, J, K, D = 4096, 256, 1024, 4, 2
 P = 128
 FLOPS = 2 * B * I * J * D
-ROWS = 4
 NT = B // P
 EPS = 1e-8
 TINY = 1e-30
-VEC_BANKS = (3,)
+XBUFS = 8
+GP_UNITS = (0, 2, 4)
 
 
 def tile_primary_capsule_t_kernel(tc, X, weight, out):
     nc = tc.nc
-    Xv = X.rearrange("(T p r) j d -> T p r (j d)", p=P, r=ROWS)
+    Xz = X.rearrange("b j d -> (b j d)").rearrange("(n R q c) -> n q R c", R=4, q=P, c=512)
     Wv = weight.rearrange("(t p) j k d -> t p (j k d)", p=P)
-    Ov = out.rearrange("(T p r) i d -> T p r (i d)", p=P, r=ROWS)
+    Ov = out.rearrange("(m e p) i d -> m p e (i d)", e=2, p=P)
     with ExitStack() as ctx:
         const = ctx.enter_context(tc.tile_pool(name="const", bufs=1))
-        xin = ctx.enter_context(tc.tile_pool(name="xin", bufs=3))
-        wtmp = ctx.enter_context(tc.tile_pool(name="wtmp", bufs=2))
-        grp = ctx.enter_context(tc.tile_pool(name="grp", bufs=4))
-        xqp = ctx.enter_context(tc.tile_pool(name="xqp", bufs=8))
-        ep = ctx.enter_context(tc.tile_pool(name="ep", bufs=3))
+        xin = ctx.enter_context(tc.tile_pool(name="xin", bufs=XBUFS))
+        wtmp = ctx.enter_context(tc.tile_pool(name="wtmp", bufs=4))
+        grp = ctx.enter_context(tc.tile_pool(name="grp", bufs=3))
+        xqp = ctx.enter_context(tc.tile_pool(name="xqp", bufs=4))
+        ep = ctx.enter_context(tc.tile_pool(name="ep", bufs=4))
+        outp = ctx.enter_context(tc.tile_pool(name="outp", bufs=3))
         tp = ctx.enter_context(tc.psum_pool(name="tp", bufs=4))
         accp = ctx.enter_context(tc.psum_pool(name="accp", bufs=4))
+        ctx.enter_context(tc.manual_schedule())
 
         warm = const.tile([P, 1], F32, name="warm")
         nc.vector.memset(warm[:], 1.0)
         nc.scalar.activation(out=warm[:], in_=warm[:], func=ACT.Abs_reciprocal_sqrt)
-
-        ident_f = const.tile([P, P], F32, name="ident_f")
-        make_identity(nc, ident_f[:])
         ident_b = const.tile([P, P], BF16, name="ident_b")
         make_identity(nc, ident_b[:])
 
-        x_tiles = {}
+        x_t = {}
+        xt_t = {}
+        gx_t = {}
+        xq_t = {}
+        acc_t = {}
+        e_t = {}
+        o_t = {}
+        done = set()
 
-        def load_x(T, split):
-            x_sb = xin.tile([P, ROWS, J * D], BF16, name="x_sb")
-            if split:
-                for r in range(ROWS):
-                    nc.sync.dma_start(out=x_sb[:, r, :], in_=Xv[T][:, r, :])
-            else:
-                nc.sync.dma_start(out=x_sb[:], in_=Xv[T])
-            x_tiles[T] = x_sb
+        def once(key):
+            if key in done:
+                return False
+            done.add(key)
+            return True
 
-        load_x(0, True)
+        def load(n):
+            if 0 <= n < NT and once(("load", n)):
+                x_sb = xin.tile([P, 4, 512], BF16, name="x_sb")
+                nc.sync.dma_start(out=x_sb[:], in_=Xz[n])
+                x_t[n] = x_sb
+
+        def transposes(n):
+            if 0 <= n < NT and once(("T", n)):
+                banks = []
+                for d in range(D):
+                    xt = tp.tile([P, 2, P, 4], BF16, name="xt", tag="tp")
+                    for R in range(4):
+                        xv = x_t[n][:, R, :].rearrange("q (t p d) -> q t p d", t=2, d=D)
+                        for t in range(2):
+                            nc.tensor.transpose(
+                                xt[:, :, 32 * R:32 * R + 32, 2 * t:2 * t + 2].rearrange("p g b h -> p b g h"),
+                                xv[:, t, :, d], ident_b[:])
+                    banks.append(xt)
+                xt_t[n] = banks
+
+        def copy(n, d):
+            if 0 <= n < NT and once(("c", n, d)):
+                if d == 0:
+                    gx_new = grp.tile([P, D, 2, P, 4], BF16, name="gx", align_bytes=64)
+                    gx_t[n] = gx_new
+                if d == 1 and n % 2 == 1:
+                    nc.vector.tensor_copy(out=gx_t[n][:, d], in_=xt_t[n][d][:])
+                else:
+                    nc.scalar.copy(out=gx_t[n][:, d], in_=xt_t[n][d][:])
+
+        def quant(n):
+            if 0 <= n < NT and once(("Q", n)):
+                xq = xqp.tile([P, 4 * P], U32, name="xq", align_bytes=64)
+                xs = xqp.tile([P, 4 * P], U8, name="xs", align_bytes=64)
+                nc.vector.quantize_mx(out=xq[:].bitcast(FP8X4), scales=xs[:],
+                                      in_=gx_t[n][:].rearrange("p d g b s -> p (d g b s)"))
+                xq_t[n] = (xq, xs)
+
+        UNIT = 256 * K * D
         w_raw = [const.tile([P, J * K * D], BF16, name="w_raw%d" % t) for t in range(2)]
-        HALF = J * K * D // 2
-        for g in range(2):
-            for t in range(2):
-                nc.sync.dma_start(out=w_raw[t][:, g * HALF:(g + 1) * HALF],
-                                  in_=Wv[t][:, g * HALF:(g + 1) * HALF])
-        load_x(1, False)
-
-        bank_no = [0]
-
-        def copy_out(dst, src):
-            if bank_no[0] % 8 in VEC_BANKS:
-                nc.vector.tensor_copy(out=dst, in_=src)
-            else:
-                nc.scalar.copy(out=dst, in_=src)
-            bank_no[0] += 1
-
-        xq_tiles = {}
-
-        def front(n):
-            T, r = divmod(n, ROWS)
-            xw = x_tiles[T][:, r, :].bitcast(F32)
-            gx = grp.tile([P, 2, D, P, 4], BF16, name="gx", align_bytes=64)
-            for g in range(2):
-                xt = tp.tile([P, 4, P], F32, name="xt", tag="tp")
-                for u in range(4):
-                    c = 4 * g + u
-                    nc.tensor.transpose(xt[:, u, :], xw[:, c * P:(c + 1) * P], ident_f[:])
-                copy_out(gx[:, g], xt[:].bitcast(BF16).rearrange("p u (b d) -> p d b u", d=D))
-            xq = xqp.tile([P, 4 * P], U32, name="xq", align_bytes=64)
-            xs = xqp.tile([P, 4 * P], U8, name="xs", align_bytes=64)
-            nc.vector.quantize_mx(out=xq[:].bitcast(FP8X4), scales=xs[:],
-                                  in_=gx[:].rearrange("p g d b t -> p (g d b t)"))
-            xq_tiles[n] = (xq, xs)
-
-        front(0)
-        front(1)
+        units = [(g, t, hf) for g in range(2) for t in range(2) for hf in range(2)]
+        for (g, t, hf) in units:
+            e0 = (2 * g + hf) * UNIT
+            nc.sync.dma_start(out=w_raw[t][:, e0:e0 + UNIT], in_=Wv[t][:, e0:e0 + UNIT])
+        for n in range(XBUFS):
+            load(n)
 
         ws = [const.tile([P, D, J], BF16, name="ws%d" % t) for t in range(2)]
         gw = const.tile([P, 2, D, I, 4], BF16, name="gw", align_bytes=64)
         wq = const.tile([P, 4 * I], U32, name="wq", align_bytes=64)
         wsc = const.tile([P, 4 * I], U8, name="wsc", align_bytes=64)
-        JH = J // 2
+        for un, (g, t, hf) in enumerate(units):
+            eng = nc.gpsimd if un in GP_UNITS else nc.vector
+            e0 = (2 * g + hf) * UNIT
+            j0 = (2 * g + hf) * 256
+            w4 = w_raw[t][:, e0:e0 + UNIT].rearrange("p (j h c) -> p j h c", h=2, c=4)
+            part = wtmp.tile([P, 256, 4], F32, name="part")
+            eng.tensor_tensor(out=part[:], in0=w4[:, :, 0, :], in1=w4[:, :, 1, :], op=ALU.add)
+            pv = part[:].rearrange("p j (e d) -> p d j e", d=D)
+            eng.tensor_tensor(out=ws[t][:, :, j0:j0 + 256], in0=pv[:, :, :, 0], in1=pv[:, :, :, 1], op=ALU.add)
         for g in range(2):
             for t in range(2):
-                w4 = w_raw[t][:, g * HALF:(g + 1) * HALF].rearrange("p (j h c) -> p j h c", h=2, c=4)
-                part = wtmp.tile([P, JH, 4], F32, name="part")
-                nc.vector.tensor_tensor(out=part[:], in0=w4[:, :, 0, :], in1=w4[:, :, 1, :], op=ALU.add)
-                pv = part[:].rearrange("p j (e d) -> p d j e", d=D)
-                nc.vector.tensor_tensor(out=ws[t][:, :, g * JH:(g + 1) * JH], in0=pv[:, :, :, 0],
-                                        in1=pv[:, :, :, 1], op=ALU.add)
                 for d in range(D):
                     wt = tp.tile([P, 4, P], BF16, name="wt", tag="tp")
-                    for u in range(4):
-                        c = 4 * g + u
-                        nc.tensor.transpose(wt[:, u, :], ws[t][:, d, c * P:(c + 1) * P], ident_b[:])
+                    for s in range(4):
+                        c = 4 * g + 2 * (s % 2) + s // 2
+                        nc.tensor.transpose(wt[:, s, :], ws[t][:, d, c * P:(c + 1) * P], ident_b[:])
                     nc.scalar.copy(out=gw[:, g, d, t * P:(t + 1) * P, :],
-                                   in_=wt[:].rearrange("p u i -> p i u"))
+                                   in_=wt[:].rearrange("p s i -> p i s"))
             nc.vector.quantize_mx(out=wq[:, g * 2 * I:(g + 1) * 2 * I].bitcast(FP8X4),
                                   scales=wsc[:, g * 2 * I:(g + 1) * 2 * I],
-                                  in_=gw[:, g].rearrange("p d i t -> p (d i t)"))
+                                  in_=gw[:, g].rearrange("p d i s -> p (d i s)"))
 
         def mx(n):
-            xq, xs = xq_tiles[n]
-            acc = accp.tile([P, D, I], F32, name="acc")
-            for d in range(D):
-                for g in range(2):
-                    cx = (2 * g + d) * P
-                    cw = (2 * g + d) * I
-                    nc.tensor.matmul_mx(out=acc[:, d, :],
-                                        lhsT=xq[:, cx:cx + P].bitcast(FP8X4),
-                                        lhsT_scale=xs[:, cx:cx + P],
-                                        rhs=wq[:, cw:cw + I].bitcast(FP8X4),
-                                        rhs_scale=wsc[:, cw:cw + I],
-                                        start=(g == 0), stop=(g == 1))
-            return acc
+            if 0 <= n < NT:
+                xq, xs = xq_t[n]
+                acc = accp.tile([P, D, I], F32, name="acc")
+                for d in range(D):
+                    for g in range(2):
+                        cx = (2 * d + g) * P
+                        cw = (2 * g + d) * I
+                        nc.tensor.matmul_mx(out=acc[:, d, :],
+                                            lhsT=xq[:, cx:cx + P].bitcast(FP8X4),
+                                            lhsT_scale=xs[:, cx:cx + P],
+                                            rhs=wq[:, cw:cw + I].bitcast(FP8X4),
+                                            rhs_scale=wsc[:, cw:cw + I],
+                                            start=(g == 0), stop=(g == 1))
+                acc_t[n] = acc
 
-        def epilogue(m, accs):
-            T, h = divmod(m, 2)
-            sq = ep.tile([P, 2, D, I], F32, name="sq")
-            for e in range(2):
-                nc.scalar.activation(out=sq[:, e], in_=accs[e][:], func=ACT.Square)
-            n2 = ep.tile([P, 2, I], F32, name="n2")
-            nc.vector.tensor_tensor(out=n2[:], in0=sq[:, :, 0, :], in1=sq[:, :, 1, :], op=ALU.add)
-            nn = ep.tile([P, 2, I], F32, name="nn")
-            nc.scalar.activation(out=nn[:], in_=n2[:], func=ACT.Abs_reciprocal_sqrt, bias=TINY, scale=1.0)
-            nc.vector.tensor_tensor(out=nn[:], in0=n2[:], in1=nn[:], op=ALU.mult)
-            den = ep.tile([P, 2, I], F32, name="den")
-            nc.vector.tensor_scalar_add(out=den[:], in0=n2[:], scalar1=1.0)
-            nc.vector.scalar_tensor_tensor(out=den[:].rearrange("p e i -> p (e i)"),
-                                           in0=nn[:].rearrange("p e i -> p (e i)"), scalar=EPS,
-                                           in1=den[:].rearrange("p e i -> p (e i)"),
-                                           op0=ALU.add, op1=ALU.mult)
-            rr = ep.tile([P, 2, I], F32, name="rr")
-            nc.scalar.activation(out=rr[:], in_=den[:], func=ACT.Abs_reciprocal_sqrt)
-            nc.scalar.activation(out=rr[:], in_=rr[:], func=ACT.Square)
-            nc.vector.tensor_tensor(out=rr[:], in0=n2[:], in1=rr[:], op=ALU.mult)
-            o_sb = ep.tile([P, 2, I, D], F32, name="o_sb")
-            for e in range(2):
-                nc.vector.tensor_tensor(out=o_sb[:, e], in0=accs[e][:].rearrange("p d i -> p i d"),
-                                        in1=rr[:, e, :].unsqueeze(2).to_broadcast([P, I, D]), op=ALU.mult)
-            nc.sync.dma_start(out=Ov[T][:, 2 * h:2 * h + 2, :],
-                              in_=o_sb[:].rearrange("p e i d -> p e (i d)"))
+        def squares(n):
+            if 0 <= n < NT:
+                sq = ep.tile([P, D, I], F32, name="sq")
+                nc.scalar.activation(out=sq[:], in_=acc_t[n][:], func=ACT.Square)
+                n2 = ep.tile([P, I], F32, name="n2")
+                nc.gpsimd.tensor_tensor(out=n2[:], in0=sq[:, 0, :], in1=sq[:, 1, :], op=ALU.add)
+                e_t[n] = {"n2": n2}
 
-        for m in range(NT // 2):
-            for n in (2 * m + 2, 2 * m + 3):
-                if n < NT:
-                    if n % ROWS == 0 and n // ROWS + 1 < NT // ROWS:
-                        load_x(n // ROWS + 1, False)
-                    front(n)
-            accs = [mx(2 * m), mx(2 * m + 1)]
-            epilogue(m, accs)
+        def one_plus(n):
+            if 0 <= n < NT:
+                den = ep.tile([P, I], F32, name="den")
+                nc.vector.tensor_scalar_add(out=den[:], in0=e_t[n]["n2"][:], scalar1=1.0)
+                e_t[n]["den"] = den
+
+        def rnorm(n):
+            if 0 <= n < NT:
+                nn = ep.tile([P, I], F32, name="nn")
+                nc.scalar.activation(out=nn[:], in_=e_t[n]["n2"][:], func=ACT.Abs_reciprocal_sqrt,
+                                     bias=TINY, scale=1.0)
+                e_t[n]["nn"] = nn
+
+        def denom(n):
+            if 0 <= n < NT:
+                n2, nn, den = e_t[n]["n2"], e_t[n]["nn"], e_t[n]["den"]
+                nc.vector.tensor_tensor(out=nn[:], in0=n2[:], in1=nn[:], op=ALU.mult)
+                nc.vector.scalar_tensor_tensor(out=den[:], in0=nn[:], scalar=EPS, in1=den[:],
+                                               op0=ALU.add, op1=ALU.mult)
+
+        def factor(n):
+            if 0 <= n < NT:
+                rr = ep.tile([P, I], F32, name="rr")
+                nc.scalar.activation(out=rr[:], in_=e_t[n]["den"][:], func=ACT.Abs_reciprocal_sqrt)
+                nc.scalar.activation(out=rr[:], in_=rr[:], func=ACT.Square)
+                nc.gpsimd.tensor_tensor(out=rr[:], in0=e_t[n]["n2"][:], in1=rr[:], op=ALU.mult)
+                e_t[n]["rr"] = rr
+
+        def final(n):
+            if 0 <= n < NT:
+                m, e = divmod(n, 2)
+                if e == 0:
+                    o_new = outp.tile([P, 2, I, D], F32, name="o_sb")
+                    o_t[m] = o_new
+                nc.vector.tensor_tensor(out=o_t[m][:, e], in0=acc_t[n][:].rearrange("p d i -> p i d"),
+                                        in1=e_t[n]["rr"][:].unsqueeze(2).to_broadcast([P, I, D]), op=ALU.mult)
+                if e == 1:
+                    nc.sync.dma_start(out=Ov[m], in_=o_t[m][:].rearrange("p e i d -> p e (i d)"))
+
+        for i in range(-4, NT + 2):
+            denom(i - 1)
+            squares(i)
+            mx(i + 1)
+            final(i - 2)
+            factor(i - 1)
+            transposes(i + 4)
+            load(i + 4 + XBUFS - 2)
+            copy(i + 3, 0)
+            quant(i + 2)
+            one_plus(i)
+            rnorm(i)
+            copy(i + 3, 1)

@@ -18,7 +18,7 @@ NT = B // P
 EPS = 1e-8
 TINY = 1e-30
 XBUFS = 8
-GP_UNITS = (0, 2, 4)
+GP_UNITS = ()
 
 
 def tile_primary_capsule_t_kernel(tc, X, weight, out):
@@ -84,7 +84,7 @@ def tile_primary_capsule_t_kernel(tc, X, weight, out):
                 if d == 0:
                     gx_new = grp.tile([P, D, 2, P, 4], BF16, name="gx", align_bytes=64)
                     gx_t[n] = gx_new
-                if d == 1 and n % 2 == 1:
+                if d == 1 and n % 2 == 2:
                     nc.vector.tensor_copy(out=gx_t[n][:, d], in_=xt_t[n][d][:])
                 else:
                     nc.scalar.copy(out=gx_t[n][:, d], in_=xt_t[n][d][:])
@@ -153,7 +153,7 @@ def tile_primary_capsule_t_kernel(tc, X, weight, out):
                 sq = ep.tile([P, D, I], F32, name="sq")
                 nc.scalar.activation(out=sq[:], in_=acc_t[n][:], func=ACT.Square)
                 n2 = ep.tile([P, I], F32, name="n2")
-                nc.gpsimd.tensor_tensor(out=n2[:], in0=sq[:, 0, :], in1=sq[:, 1, :], op=ALU.add)
+                nc.vector.tensor_tensor(out=n2[:], in0=sq[:, 0, :], in1=sq[:, 1, :], op=ALU.add)
                 e_t[n] = {"n2": n2}
 
         def one_plus(n):
@@ -181,7 +181,7 @@ def tile_primary_capsule_t_kernel(tc, X, weight, out):
                 rr = ep.tile([P, I], F32, name="rr")
                 nc.scalar.activation(out=rr[:], in_=e_t[n]["den"][:], func=ACT.Abs_reciprocal_sqrt)
                 nc.scalar.activation(out=rr[:], in_=rr[:], func=ACT.Square)
-                nc.gpsimd.tensor_tensor(out=rr[:], in0=e_t[n]["n2"][:], in1=rr[:], op=ALU.mult)
+                nc.vector.tensor_tensor(out=rr[:], in0=e_t[n]["n2"][:], in1=rr[:], op=ALU.mult)
                 e_t[n]["rr"] = rr
 
         def final(n):

@@ -84,10 +84,8 @@ def tile_primary_capsule_t_kernel(tc, X, weight, out):
                 if d == 0:
                     gx_new = grp.tile([P, D, 2, P, 4], BF16, name="gx", align_bytes=64)
                     gx_t[n] = gx_new
-                if d == 1 and n % 2 == 2:
-                    nc.vector.tensor_copy(out=gx_t[n][:, d], in_=xt_t[n][d][:])
-                else:
-                    nc.scalar.copy(out=gx_t[n][:, d], in_=xt_t[n][d][:])
+                nc.scalar.copy(out=gx_t[n][:, d].rearrange("p g b s -> p (g b s)").bitcast(F32),
+                               in_=xt_t[n][d][:].rearrange("p g b s -> p (g b s)").bitcast(F32))
 
         def quant(n):
             if 0 <= n < NT and once(("Q", n)):

@@ -150,9 +150,14 @@ def tile_primary_capsule_t_kernel(tc, X, weight, out):
             if 0 <= n < NT:
                 sq = ep.tile([P, D, I], F32, name="sq")
                 nc.scalar.activation(out=sq[:], in_=acc_t[n][:], func=ACT.Square)
+                e_t[n] = {"sq": sq}
+
+        def add_squares(n):
+            if 0 <= n < NT:
+                sq = e_t[n]["sq"]
                 n2 = ep.tile([P, I], F32, name="n2")
                 nc.vector.tensor_tensor(out=n2[:], in0=sq[:, 0, :], in1=sq[:, 1, :], op=ALU.add)
-                e_t[n] = {"n2": n2}
+                e_t[n]["n2"] = n2
 
         def one_plus(n):
             if 0 <= n < NT:
@@ -179,12 +184,13 @@ def tile_primary_capsule_t_kernel(tc, X, weight, out):
                 rr = ep.tile([P, I], F32, name="rr")
                 nc.scalar.activation(out=rr[:], in_=e_t[n]["den"][:], func=ACT.Abs_reciprocal_sqrt)
                 nc.scalar.activation(out=rr[:], in_=rr[:], func=ACT.Square)
-                nc.vector.tensor_tensor(out=rr[:], in0=e_t[n]["n2"][:], in1=rr[:], op=ALU.mult)
                 e_t[n]["rr"] = rr
 
         def final(n):
             if 0 <= n < NT:
                 m, e = divmod(n, 2)
+                rr = e_t[n]["rr"]
+                nc.vector.tensor_tensor(out=rr[:], in0=e_t[n]["n2"][:], in1=rr[:], op=ALU.mult)
                 if e == 0:
                     o_new = outp.tile([P, 2, I, D], F32, name="o_sb")
                     o_t[m] = o_new
@@ -194,15 +200,16 @@ def tile_primary_capsule_t_kernel(tc, X, weight, out):
                     nc.sync.dma_start(out=Ov[m], in_=o_t[m][:].rearrange("p e i d -> p e (i d)"))
 
         for i in range(-4, NT + 2):
-            denom(i - 1)
             squares(i)
-            mx(i + 1)
-            final(i - 2)
-            factor(i - 1)
-            transposes(i + 4)
-            load(i + 4 + XBUFS - 2)
-            copy(i + 3, 0)
+            factor(i - 2)
             quant(i + 2)
-            one_plus(i)
-            rnorm(i)
+            copy(i + 3, 0)
             copy(i + 3, 1)
+            load(i + 4 + XBUFS - 2)
+            add_squares(i)
+            denom(i - 1)
+            mx(i + 1)
+            transposes(i + 4)
+            rnorm(i)
+            final(i - 2)
+            one_plus(i)

@@ -36,7 +36,6 @@ def tile_primary_capsule_t_kernel(tc, X, weight, out):
         outp = ctx.enter_context(tc.tile_pool(name="outp", bufs=3))
         tp = ctx.enter_context(tc.psum_pool(name="tp", bufs=4))
         accp = ctx.enter_context(tc.psum_pool(name="accp", bufs=4))
-        ctx.enter_context(tc.manual_schedule())
 
         warm = const.tile([P, 1], F32, name="warm")
         nc.vector.memset(warm[:], 1.0)

@@ -29,7 +29,7 @@ def tile_primary_capsule_t_kernel(tc, X, weight, out):
     with ExitStack() as ctx:
         const = ctx.enter_context(tc.tile_pool(name="const", bufs=1))
         xin = ctx.enter_context(tc.tile_pool(name="xin", bufs=XBUFS))
-        wtmp = ctx.enter_context(tc.tile_pool(name="wtmp", bufs=4))
+        wtmp = ctx.enter_context(tc.tile_pool(name="wtmp", bufs=8))
         grp = ctx.enter_context(tc.tile_pool(name="grp", bufs=3))
         xqp = ctx.enter_context(tc.tile_pool(name="xqp", bufs=4))
         ep = ctx.enter_context(tc.tile_pool(name="ep", bufs=4))
@@ -42,6 +42,8 @@ def tile_primary_capsule_t_kernel(tc, X, weight, out):
         nc.scalar.activation(out=warm[:], in_=warm[:], func=ACT.Abs_reciprocal_sqrt)
         ident_b = const.tile([P, P], BF16, name="ident_b")
         make_identity(nc, ident_b[:])
+        ident_f = const.tile([P, P], F32, name="ident_f")
+        make_identity(nc, ident_f[:])
 
         x_t = {}
         xt_t = {}
@@ -103,26 +105,27 @@ def tile_primary_capsule_t_kernel(tc, X, weight, out):
         for n in range(XBUFS):
             load(n)
 
-        ws = [const.tile([P, D, J], BF16, name="ws%d" % t) for t in range(2)]
         gw = const.tile([P, 2, D, I, 4], BF16, name="gw", align_bytes=64)
         wq = const.tile([P, 4 * I], U32, name="wq", align_bytes=64)
         wsc = const.tile([P, 4 * I], U8, name="wsc", align_bytes=64)
-        for un, (g, t, hf) in enumerate(units):
-            eng = nc.gpsimd if un in GP_UNITS else nc.vector
+        parts = {}
+        for (g, t, hf) in units:
             e0 = (2 * g + hf) * UNIT
-            j0 = (2 * g + hf) * 256
             w4 = w_raw[t][:, e0:e0 + UNIT].rearrange("p (j h c) -> p j h c", h=2, c=4)
-            part = wtmp.tile([P, 256, 4], F32, name="part")
-            eng.tensor_tensor(out=part[:], in0=w4[:, :, 0, :], in1=w4[:, :, 1, :], op=ALU.add)
-            pv = part[:].rearrange("p j (e d) -> p d j e", d=D)
-            eng.tensor_tensor(out=ws[t][:, :, j0:j0 + 256], in0=pv[:, :, :, 0], in1=pv[:, :, :, 1], op=ALU.add)
+            part = wtmp.tile([P, 4, 256], F32, name="part")
+            nc.vector.tensor_tensor(out=part[:].rearrange("p c j -> p j c"), in0=w4[:, :, 0, :],
+                                    in1=w4[:, :, 1, :], op=ALU.add)
+            parts[(g, t, hf)] = part
         for g in range(2):
             for t in range(2):
                 for d in range(D):
-                    wt = tp.tile([P, 4, P], BF16, name="wt", tag="tp")
+                    wt = tp.tile([P, 4, P], F32, name="wt", tag="tp")
                     for s in range(4):
-                        c = 4 * g + 2 * (s % 2) + s // 2
-                        nc.tensor.transpose(wt[:, s, :], ws[t][:, d, c * P:(c + 1) * P], ident_b[:])
+                        hf, q = s % 2, s // 2
+                        for e in range(2):
+                            nc.tensor.matmul(out=wt[:, s, :],
+                                             lhsT=parts[(g, t, hf)][:, 2 * e + d, q * P:(q + 1) * P],
+                                             rhs=ident_f[:], start=(e == 0), stop=(e == 1), is_transpose=True)
                     nc.scalar.copy(out=gw[:, g, d, t * P:(t + 1) * P, :],
                                    in_=wt[:].rearrange("p s i -> p i s"))
             nc.vector.quantize_mx(out=wq[:, g * 2 * I:(g + 1) * 2 * I].bitcast(FP8X4),

@@ -25,7 +25,7 @@ def tile_primary_capsule_t_kernel(tc, X, weight, out):
     nc = tc.nc
     Xz = X.rearrange("b j d -> (b j d)").rearrange("(n R q c) -> n q R c", R=4, q=P, c=512)
     Wv = weight.rearrange("(t p) j k d -> t p (j k d)", p=P)
-    Ov = out.rearrange("(m e p) i d -> m p e (i d)", e=2, p=P)
+    Ov = out.rearrange("(n p) i d -> n p (i d)", p=P)
     with ExitStack() as ctx:
         const = ctx.enter_context(tc.tile_pool(name="const", bufs=1))
         xin = ctx.enter_context(tc.tile_pool(name="xin", bufs=XBUFS))
@@ -33,7 +33,7 @@ def tile_primary_capsule_t_kernel(tc, X, weight, out):
         grp = ctx.enter_context(tc.tile_pool(name="grp", bufs=3))
         xqp = ctx.enter_context(tc.tile_pool(name="xqp", bufs=4))
         ep = ctx.enter_context(tc.tile_pool(name="ep", bufs=4))
-        outp = ctx.enter_context(tc.tile_pool(name="outp", bufs=3))
+        outp = ctx.enter_context(tc.tile_pool(name="outp", bufs=4))
         tp = ctx.enter_context(tc.psum_pool(name="tp", bufs=4))
         accp = ctx.enter_context(tc.psum_pool(name="accp", bufs=4))
 
@@ -99,6 +99,7 @@ def tile_primary_capsule_t_kernel(tc, X, weight, out):
         UNIT = 256 * K * D
         w_raw = [const.tile([P, J * K * D], BF16, name="w_raw%d" % t) for t in range(2)]
         units = [(g, t, hf) for g in range(2) for t in range(2) for hf in range(2)]
+        load(0)
         for (g, t, hf) in units:
             e0 = (2 * g + hf) * UNIT
             nc.sync.dma_start(out=w_raw[t][:, e0:e0 + UNIT], in_=Wv[t][:, e0:e0 + UNIT])
@@ -126,8 +127,12 @@ def tile_primary_capsule_t_kernel(tc, X, weight, out):
                             nc.tensor.matmul(out=wt[:, s, :],
                                              lhsT=parts[(g, t, hf)][:, 2 * e + d, q * P:(q + 1) * P],
                                              rhs=ident_f[:], start=(e == 0), stop=(e == 1), is_transpose=True)
-                    nc.scalar.copy(out=gw[:, g, d, t * P:(t + 1) * P, :],
-                                   in_=wt[:].rearrange("p s i -> p i s"))
+                    if d == 0:
+                        nc.scalar.copy(out=gw[:, g, d, t * P:(t + 1) * P, :],
+                                       in_=wt[:].rearrange("p s i -> p i s"))
+                    else:
+                        nc.vector.tensor_copy(out=gw[:, g, d, t * P:(t + 1) * P, :],
+                                              in_=wt[:].rearrange("p s i -> p i s"))
             nc.vector.quantize_mx(out=wq[:, g * 2 * I:(g + 1) * 2 * I].bitcast(FP8X4),
                                   scales=wsc[:, g * 2 * I:(g + 1) * 2 * I],
                                   in_=gw[:, g].rearrange("p d i s -> p (d i s)"))
@@ -193,13 +198,10 @@ def tile_primary_capsule_t_kernel(tc, X, weight, out):
                 m, e = divmod(n, 2)
                 rr = e_t[n]["rr"]
                 nc.vector.tensor_tensor(out=rr[:], in0=e_t[n]["n2"][:], in1=rr[:], op=ALU.mult)
-                if e == 0:
-                    o_new = outp.tile([P, 2, I, D], F32, name="o_sb")
-                    o_t[m] = o_new
-                nc.vector.tensor_tensor(out=o_t[m][:, e], in0=acc_t[n][:].rearrange("p d i -> p i d"),
+                o_sb = outp.tile([P, I, D], F32, name="o_sb")
+                nc.vector.tensor_tensor(out=o_sb[:], in0=acc_t[n][:].rearrange("p d i -> p i d"),
                                         in1=e_t[n]["rr"][:].unsqueeze(2).to_broadcast([P, I, D]), op=ALU.mult)
-                if e == 1:
-                    nc.sync.dma_start(out=Ov[m], in_=o_t[m][:].rearrange("p e i d -> p e (i d)"))
+                nc.sync.dma_start(out=Ov[n], in_=o_sb[:].rearrange("p i d -> p (i d)"))
 
         for i in range(-4, NT + 2):
             squares(i)

from contextlib import ExitStack

import concourse.mybir as mybir
from concourse.masks import make_identity

F32 = mybir.dt.float32
BF16 = mybir.dt.bfloat16
U32 = mybir.dt.uint32
U8 = mybir.dt.uint8
FP8X4 = mybir.dt.float8_e4m3fn_x4
ACT = mybir.ActivationFunctionType
ALU = mybir.AluOpType

B, I, J, K, D = 4096, 256, 1024, 4, 2
P = 128
FLOPS = 2 * B * I * J * D
NT = B // P
EPS = 1e-8
TINY = 1e-30
XBUFS = 8
GP_UNITS = ()


def tile_primary_capsule_t_kernel(tc, X, weight, out):
    nc = tc.nc
    Xz = X.rearrange("b j d -> (b j d)").rearrange("(n R q c) -> n q R c", R=4, q=P, c=512)
    Wv = weight.rearrange("(t p) j k d -> t p (j k d)", p=P)
    Ov = out.rearrange("(n p) i d -> n p (i d)", p=P)
    with ExitStack() as ctx:
        const = ctx.enter_context(tc.tile_pool(name="const", bufs=1))
        xin = ctx.enter_context(tc.tile_pool(name="xin", bufs=XBUFS))
        wtmp = ctx.enter_context(tc.tile_pool(name="wtmp", bufs=8))
        grp = ctx.enter_context(tc.tile_pool(name="grp", bufs=3))
        xqp = ctx.enter_context(tc.tile_pool(name="xqp", bufs=4))
        ep = ctx.enter_context(tc.tile_pool(name="ep", bufs=4))
        outp = ctx.enter_context(tc.tile_pool(name="outp", bufs=4))
        tp = ctx.enter_context(tc.psum_pool(name="tp", bufs=4))
        accp = ctx.enter_context(tc.psum_pool(name="accp", bufs=4))

        warm = const.tile([P, 1], F32, name="warm")
        nc.vector.memset(warm[:], 1.0)
        nc.scalar.activation(out=warm[:], in_=warm[:], func=ACT.Abs_reciprocal_sqrt)
        ident_b = const.tile([P, P], BF16, name="ident_b")
        make_identity(nc, ident_b[:])
        ident_f = const.tile([P, P], F32, name="ident_f")
        make_identity(nc, ident_f[:])

        x_t = {}
        xt_t = {}
        gx_t = {}
        xq_t = {}
        acc_t = {}
        e_t = {}
        o_t = {}
        done = set()

        def once(key):
            if key in done:
                return False
            done.add(key)
            return True

        def load(n):
            if 0 <= n < NT and once(("load", n)):
                x_sb = xin.tile([P, 4, 512], BF16, name="x_sb")
                nc.sync.dma_start(out=x_sb[:], in_=Xz[n])
                x_t[n] = x_sb

        def transposes(n):
            if 0 <= n < NT and once(("T", n)):
                banks = []
                for d in range(D):
                    xt = tp.tile([P, 2, P, 4], BF16, name="xt", tag="tp")
                    for R in range(4):
                        xv = x_t[n][:, R, :].rearrange("q (t p d) -> q t p d", t=2, d=D)
                        for t in range(2):
                            nc.tensor.transpose(
                                xt[:, :, 32 * R:32 * R + 32, 2 * t:2 * t + 2].rearrange("p g b h -> p b g h"),
                                xv[:, t, :, d], ident_b[:])
                    banks.append(xt)
                xt_t[n] = banks

        def copy(n, d):
            if 0 <= n < NT and once(("c", n, d)):
                if d == 0:
                    gx_new = grp.tile([P, D, 2, P, 4], BF16, name="gx", align_bytes=64)
                    gx_t[n] = gx_new
                nc.scalar.copy(out=gx_t[n][:, d].rearrange("p g b s -> p (g b s)").bitcast(F32),
                               in_=xt_t[n][d][:].rearrange("p g b s -> p (g b s)").bitcast(F32))

        def quant(n):
            if 0 <= n < NT and once(("Q", n)):
                xq = xqp.tile([P, 4 * P], U32, name="xq", align_bytes=64)
                xs = xqp.tile([P, 4 * P], U8, name="xs", align_bytes=64)
                nc.vector.quantize_mx(out=xq[:].bitcast(FP8X4), scales=xs[:],
                                      in_=gx_t[n][:].rearrange("p d g b s -> p (d g b s)"))
                xq_t[n] = (xq, xs)

        UNIT = 256 * K * D
        w_raw = [const.tile([P, J * K * D], BF16, name="w_raw%d" % t) for t in range(2)]
        units = [(g, t, hf) for g in range(2) for t in range(2) for hf in range(2)]
        load(0)
        for (g, t, hf) in units:
            e0 = (2 * g + hf) * UNIT
            nc.sync.dma_start(out=w_raw[t][:, e0:e0 + UNIT], in_=Wv[t][:, e0:e0 + UNIT])
        for n in range(XBUFS):
            load(n)

        gw = const.tile([P, 2, D, I, 4], BF16, name="gw", align_bytes=64)
        wq = const.tile([P, 4 * I], U32, name="wq", align_bytes=64)
        wsc = const.tile([P, 4 * I], U8, name="wsc", align_bytes=64)
        parts = {}
        for (g, t, hf) in units:
            e0 = (2 * g + hf) * UNIT
            w4 = w_raw[t][:, e0:e0 + UNIT].rearrange("p (j h c) -> p j h c", h=2, c=4)
            part = wtmp.tile([P, 4, 256], F32, name="part")
            nc.vector.tensor_tensor(out=part[:].rearrange("p c j -> p j c"), in0=w4[:, :, 0, :],
                                    in1=w4[:, :, 1, :], op=ALU.add)
            parts[(g, t, hf)] = part
        for g in range(2):
            for t in range(2):
                for d in range(D):
                    wt = tp.tile([P, 4, P], F32, name="wt", tag="tp")
                    for s in range(4):
                        hf, q = s % 2, s // 2
                        for e in range(2):
                            nc.tensor.matmul(out=wt[:, s, :],
                                             lhsT=parts[(g, t, hf)][:, 2 * e + d, q * P:(q + 1) * P],
                                             rhs=ident_f[:], start=(e == 0), stop=(e == 1), is_transpose=True)
                    if d == 0:
                        nc.scalar.copy(out=gw[:, g, d, t * P:(t + 1) * P, :],
                                       in_=wt[:].rearrange("p s i -> p i s"))
                    else:
                        nc.vector.tensor_copy(out=gw[:, g, d, t * P:(t + 1) * P, :],
                                              in_=wt[:].rearrange("p s i -> p i s"))
            nc.vector.quantize_mx(out=wq[:, g * 2 * I:(g + 1) * 2 * I].bitcast(FP8X4),
                                  scales=wsc[:, g * 2 * I:(g + 1) * 2 * I],
                                  in_=gw[:, g].rearrange("p d i s -> p (d i s)"))

        def mx(n):
            if 0 <= n < NT:
                xq, xs = xq_t[n]
                acc = accp.tile([P, D, I], F32, name="acc")
                for d in range(D):
                    for g in range(2):
                        cx = (2 * d + g) * P
                        cw = (2 * g + d) * I
                        nc.tensor.matmul_mx(out=acc[:, d, :],
                                            lhsT=xq[:, cx:cx + P].bitcast(FP8X4),
                                            lhsT_scale=xs[:, cx:cx + P],
                                            rhs=wq[:, cw:cw + I].bitcast(FP8X4),
                                            rhs_scale=wsc[:, cw:cw + I],
                                            start=(g == 0), stop=(g == 1))
                acc_t[n] = acc

        def squares(n):
            if 0 <= n < NT:
                sq = ep.tile([P, D, I], F32, name="sq")
                nc.scalar.activation(out=sq[:], in_=acc_t[n][:], func=ACT.Square)
                e_t[n] = {"sq": sq}

        def add_squares(n):
            if 0 <= n < NT:
                sq = e_t[n]["sq"]
                n2 = ep.tile([P, I], F32, name="n2")
                nc.vector.tensor_tensor(out=n2[:], in0=sq[:, 0, :], in1=sq[:, 1, :], op=ALU.add)
                e_t[n]["n2"] = n2

        def one_plus(n):
            if 0 <= n < NT:
                den = ep.tile([P, I], F32, name="den")
                nc.vector.tensor_scalar_add(out=den[:], in0=e_t[n]["n2"][:], scalar1=1.0)
                e_t[n]["den"] = den

        def rnorm(n):
            if 0 <= n < NT:
                nn = ep.tile([P, I], F32, name="nn")
                nc.scalar.activation(out=nn[:], in_=e_t[n]["n2"][:], func=ACT.Abs_reciprocal_sqrt,
                                     bias=TINY, scale=1.0)
                e_t[n]["nn"] = nn

        def denom(n):
            if 0 <= n < NT:
                n2, nn, den = e_t[n]["n2"], e_t[n]["nn"], e_t[n]["den"]
                nc.vector.tensor_tensor(out=nn[:], in0=n2[:], in1=nn[:], op=ALU.mult)
                nc.vector.scalar_tensor_tensor(out=den[:], in0=nn[:], scalar=EPS, in1=den[:],
                                               op0=ALU.add, op1=ALU.mult)

        def factor(n):
            if 0 <= n < NT:
                rr = ep.tile([P, I], F32, name="rr")
                nc.scalar.activation(out=rr[:], in_=e_t[n]["den"][:], func=ACT.Abs_reciprocal_sqrt)
                nc.scalar.activation(out=rr[:], in_=rr[:], func=ACT.Square)
                e_t[n]["rr"] = rr

        def final(n):
            if 0 <= n < NT:
                m, e = divmod(n, 2)
                rr = e_t[n]["rr"]
                nc.vector.tensor_tensor(out=rr[:], in0=e_t[n]["n2"][:], in1=rr[:], op=ALU.mult)
                o_sb = outp.tile([P, I, D], F32, name="o_sb")
                nc.vector.tensor_tensor(out=o_sb[:], in0=acc_t[n][:].rearrange("p d i -> p i d"),
                                        in1=e_t[n]["rr"][:].unsqueeze(2).to_broadcast([P, I, D]), op=ALU.mult)
                nc.sync.dma_start(out=Ov[n], in_=o_sb[:].rearrange("p i d -> p (i d)"))

        for i in range(-4, NT + 2):
            squares(i)
            factor(i - 2)
            quant(i + 2)
            copy(i + 3, 0)
            copy(i + 3, 1)
            load(i + 4 + XBUFS - 2)
            add_squares(i)
            denom(i - 1)
            mx(i + 1)
            transposes(i + 4)
            rnorm(i)
            final(i - 2)
            one_plus(i)
